import numpy as np
import ml_dtypes


def mxq(x, axis, fmt="e4m3"):
    dtype, down = {"e4m3": (ml_dtypes.float8_e4m3fn, 7), "e5m2": (ml_dtypes.float8_e5m2, 14)}[fmt]
    v = np.moveaxis(np.asarray(x, np.float32).astype(ml_dtypes.bfloat16).astype(np.float64), axis, -1)
    blocks = v.reshape(v.shape[:-1] + (-1, 32))
    amax = np.abs(blocks).max(-1, keepdims=True)
    byte = np.maximum(np.where(amax > 0, np.frexp(amax)[1] - 1 + 127, 0) - down, 1)
    scale = np.exp2(byte - 127.0)
    codes = (blocks / scale).astype(np.float32).astype(dtype).astype(np.float64)
    return np.moveaxis((codes * scale).reshape(v.shape), -1, axis)


WIDE = False


def mx_kscale(k):
    if not WIDE:
        return np.ones(k)
    levels = np.array([10, -10, 5, -5, 0])
    a = np.random.permutation(np.resize(levels, k // 512 * 4)).reshape(k // 512, 4)
    idx = np.arange(k)
    return np.exp2(a[idx // 512, idx % 128 // 32])


BF16 = ml_dtypes.bfloat16


def bf(x):
    return np.asarray(x, np.float32).astype(BF16)


def f64(x):
    return np.asarray(x).astype(np.float64)


N, L, D, M = 512, 32, 512, 512


def l2norm(v):
    n = np.sqrt((v * v).sum(axis=-1, keepdims=True))
    return v / np.maximum(n, 1e-12)


def setup_inputs():
    s = mx_kscale(D)
    amp_f = 0.5 + 1.5 * np.random.random((N, L))[:, :, None]
    amp_v = 0.5 + 1.5 * np.random.random(N)[:, None]
    return {"feature": bf(np.random.standard_normal((N, L, D)) * amp_f * s),
            "aspect_v": bf(np.random.standard_normal((N, D)) * amp_v * s),
            "W": bf(np.random.standard_normal((M, D)) * np.sqrt(2.0 / (D + M)) / s),
            "b": bf(np.random.standard_normal(M) * 0.2)}


def reference(feature, aspect_v, W, b):
    wq = mxq(f64(W), 1, "e4m3")
    q = l2norm((mxq(f64(aspect_v), 1, "e4m3") @ wq.T) + f64(b))
    fn = l2norm((mxq(f64(feature), 2, "e4m3") @ wq.T) + f64(b))
    return q, fn.mean(axis=1)

@@ -1,0 +1,276 @@
+from contextlib import ExitStack
+
+import concourse.mybir as mybir
+from concourse.masks import make_identity
+
+F32 = mybir.dt.float32
+BF16 = mybir.dt.bfloat16
+U32 = mybir.dt.uint32
+U8 = mybir.dt.uint8
+FP8X4 = mybir.dt.float8_e4m3fn_x4
+ADD = mybir.AluOpType.add
+MULT = mybir.AluOpType.mult
+SQUARE = mybir.ActivationFunctionType.Square
+
+P = 128
+D_IN = 512
+D_OUT = 512
+TOKENS = 32
+TILES = 4
+FOLDED = 2
+KEPT = TILES - FOLDED
+assert FOLDED <= KEPT
+BATCH_ROWS = TILES * P
+GROUP_BATCHES = 2
+GROUP_TILES = GROUP_BATCHES * TILES
+GROUP_ROWS = GROUP_TILES * P
+GROUP_SEGMENTS = GROUP_ROWS // TOKENS
+SEGMENT_PARTITIONS = TOKENS // GROUP_TILES
+BLOCK_GROUPS = P // GROUP_SEGMENTS
+BLOCK_BATCHES = BLOCK_GROUPS * GROUP_BATCHES
+OUT_SLICES = D_OUT // P
+BATCH_SLICES = OUT_SLICES // GROUP_BATCHES
+WORDS = D_IN // 2
+BANK_TILES = 2
+BANKS = TILES // BANK_TILES
+LOOKAHEAD = 4
+SUM_LAG = 3
+TINY = 1e-24
+
+FLOPS = 2 * (512 * 32 + 512) * D_IN * D_OUT
+
+
+def tile_linearattention_pa_t_kernel(tc, feature, aspect_v, W, b, out_0, out_1):
+    nc = tc.nc
+    tokens = feature.flatten_outer_dims()
+    feature_batches = tokens.shape[0] // BATCH_ROWS
+    aspect_batch = feature_batches
+    batches = feature_batches + 1
+
+    with ExitStack() as ctx:
+        ctx.enter_context(tc.manual_schedule())
+        const = ctx.enter_context(tc.tile_pool(name="const", bufs=1))
+        rows_pool = ctx.enter_context(tc.tile_pool(name="rows", bufs=LOOKAHEAD))
+        grouped_pool = ctx.enter_context(tc.tile_pool(name="grouped", bufs=2 * BANKS))
+        codes_pool = ctx.enter_context(tc.tile_pool(name="codes", bufs=2))
+        y_pool = ctx.enter_context(tc.tile_pool(name="y", bufs=(SUM_LAG + GROUP_BATCHES + 1) * TILES))
+        weights_pool = ctx.enter_context(tc.tile_pool(name="weights", bufs=SUM_LAG + GROUP_BATCHES + 1))
+        squares_pool = ctx.enter_context(tc.tile_pool(name="squares", bufs=TILES))
+        norm_pool = ctx.enter_context(tc.tile_pool(name="norm", bufs=3))
+        fm_pool = ctx.enter_context(tc.tile_pool(name="fm", bufs=2))
+        words_psum = ctx.enter_context(tc.psum_pool(name="words_psum", bufs=BANKS))
+        product_psum = ctx.enter_context(tc.psum_pool(name="product_psum", bufs=TILES))
+        fm_t_psum = ctx.enter_context(tc.psum_pool(name="fm_t_psum", bufs=1))
+        fm_psum = ctx.enter_context(tc.psum_pool(name="fm_psum", bufs=1))
+
+        rows_of = {}
+        banks_of = {}
+        grouped_of = {}
+        codes_of = {}
+        scales_of = {}
+        y_of = {}
+        sumsq_of = {}
+        norm_of = {}
+        weights_of = {}
+        ratio_of = {}
+        fm_t_of = {}
+        fm_t_sbuf_of = {}
+
+        def load(n, dram_view):
+            rows = rows_pool.tile([P, TILES * D_IN], BF16, name="rows")
+            nc.sync.dma_start(out=rows[:].rearrange("p (j k) -> p j k", j=TILES), in_=dram_view)
+            rows_of[n] = rows
+
+        def load_batch(n):
+            if n == aspect_batch:
+                load(n, aspect_v.rearrange("(p j) k -> p j k", j=TILES))
+            else:
+                group, part = divmod(n, GROUP_BATCHES)
+                group_rows = tokens[group * GROUP_ROWS : (group + 1) * GROUP_ROWS, :]
+                by_partition = group_rows.rearrange("(p j) k -> p j k", j=GROUP_TILES)
+                load(n, by_partition[:, part * TILES : (part + 1) * TILES, :])
+
+        def transpose(n):
+            words = rows_of[n][:].bitcast(F32)
+            blocks = BANK_TILES * WORDS // P
+            banks_of[n] = []
+            for h in range(BANKS):
+                bank = words_psum.tile([P, BANK_TILES * WORDS], F32, name="bank")
+                for block in range(blocks):
+                    nc.tensor.transpose(
+                        out=bank[:, block * P : (block + 1) * P],
+                        in_=words[:, (h * blocks + block) * P : (h * blocks + block + 1) * P],
+                        identity=identity[:],
+                    )
+                banks_of[n].append(bank)
+
+        def regroup(n):
+            grouped_of[n] = []
+            for bank in banks_of[n]:
+                grouped = grouped_pool.tile([P, BANK_TILES * P * 4], BF16, name="grouped", align_bytes=64)
+                nc.scalar.copy(
+                    out=grouped[:].bitcast(F32).rearrange("p (j r u) -> p j r u", j=BANK_TILES, u=2),
+                    in_=bank[:].rearrange("p (j u r) -> p j r u", j=BANK_TILES, u=2),
+                )
+                grouped_of[n].append(grouped)
+
+        def new_codes(n, pool):
+            codes = pool.tile([P, TILES * P], U32, name="codes", align_bytes=64)
+            scales = pool.tile([P, TILES * P], U8, name="scales", align_bytes=64)
+            codes_of[n] = codes
+            scales_of[n] = scales
+
+        def quantise(n, h):
+            cols = slice(h * BANK_TILES * P, (h + 1) * BANK_TILES * P)
+            nc.vector.quantize_mx(
+                out=codes_of[n][:, cols].bitcast(FP8X4),
+                scales=scales_of[n][:, cols],
+                in_=grouped_of[n][h][:],
+            )
+
+        def multiply(n, j):
+            if j == 0:
+                sumsq = norm_pool.tile([P, TILES], F32, name="sumsq")
+                sumsq_of[n] = sumsq
+            cols = slice(j * P, (j + 1) * P)
+            product = product_psum.tile([P, D_OUT], F32, name="product")
+            nc.tensor.matmul_mx(
+                out=product[:],
+                lhsT=codes_of[n][:, cols].bitcast(FP8X4),
+                lhsT_scale=scales_of[n][:, cols],
+                rhs=codes_of["W"][:].bitcast(FP8X4),
+                rhs_scale=scales_of["W"][:],
+                start=True,
+                stop=True,
+            )
+            y = y_pool.tile([P, D_OUT], F32, name="y")
+            y_of[n, j] = y
+            nc.vector.tensor_tensor(out=y[:], in0=product[:], in1=bias[:], op=ADD)
+            squares = squares_pool.tile([P, D_OUT], BF16, name="squares")
+            nc.scalar.activation(out=squares[:], in_=y[:], func=SQUARE, accum_out=sumsq_of[n][:, j : j + 1])
+
+        def norms(n):
+            floored = norm_pool.tile([P, TILES], F32, name="floored")
+            norm = norm_pool.tile([P, TILES], F32, name="norm")
+            nc.vector.tensor_scalar_max(out=floored[:], in0=sumsq_of[n][:], scalar1=TINY)
+            nc.scalar.sqrt(out=norm[:], in_=floored[:])
+            norm_of[n] = norm
+
+        def token_weights(n):
+            inverse = norm_pool.tile([P, TILES], F32, name="inverse")
+            ratio = norm_pool.tile([P, FOLDED], F32, name="ratio")
+            weights = weights_pool.tile([P, KEPT, GROUP_SEGMENTS], F32, name="weights")
+            nc.vector.reciprocal(out=inverse[:], in_=norm_of[n][:])
+            nc.vector.tensor_tensor(out=ratio[:], in0=inverse[:, KEPT:], in1=norm_of[n][:, :FOLDED], op=MULT)
+            nc.vector.tensor_tensor(
+                out=weights[:],
+                in0=membership[:].unsqueeze(1).to_broadcast([P, KEPT, GROUP_SEGMENTS]),
+                in1=inverse[:, :KEPT].unsqueeze(2).to_broadcast([P, KEPT, GROUP_SEGMENTS]),
+                op=MULT,
+            )
+            weights_of[n] = weights
+            ratio_of[n] = ratio
+
+        def fold(n, i):
+            kept = y_of[n, i]
+            nc.vector.scalar_tensor_tensor(
+                out=kept[:], in0=y_of[n, KEPT + i][:], scalar=ratio_of[n][:, i : i + 1], in1=kept[:], op0=MULT, op1=ADD
+            )
+
+        def reduce_tokens(group, s):
+            block, place = divmod(group, BLOCK_GROUPS)
+            if place == 0 and s == 0:
+                fm_t = fm_t_psum.tile([P, OUT_SLICES * P], F32, name="fm_t")
+                fm_t_of[block] = fm_t
+            first = s * P + place * GROUP_SEGMENTS
+            for tile in range(GROUP_BATCHES * KEPT):
+                part, j = divmod(tile, KEPT)
+                n = group * GROUP_BATCHES + part
+                nc.tensor.matmul(
+                    out=fm_t_of[block][:, first : first + GROUP_SEGMENTS],
+                    lhsT=y_of[n, j][:, s * P : (s + 1) * P],
+                    rhs=weights_of[n][:, j, :],
+                    start=(tile == 0),
+                    stop=(tile == GROUP_BATCHES * KEPT - 1),
+                )
+
+        def collect_block(block):
+            fm_t_sbuf = fm_pool.tile([P, OUT_SLICES * P], F32, name="fm_t_sbuf")
+            nc.vector.tensor_copy(out=fm_t_sbuf[:], in_=fm_t_of[block][:])
+            fm_t_sbuf_of[block] = fm_t_sbuf
+
+        def store_block(block):
+            fm_bank = fm_psum.tile([P, D_OUT], F32, name="fm_bank")
+            for s in range(OUT_SLICES):
+                cols = slice(s * P, (s + 1) * P)
+                nc.tensor.transpose(out=fm_bank[:, cols], in_=fm_t_sbuf_of[block][:, cols], identity=identity[:])
+            fm = fm_pool.tile([P, D_OUT], F32, name="fm")
+            nc.scalar.copy(out=fm[:], in_=fm_bank[:])
+            nc.sync.dma_start(out=out_1[block * P : (block + 1) * P, :], in_=fm[:])
+
+        def store_q(n):
+            inverse = norm_pool.tile([P, TILES], F32, name="inverse")
+            nc.vector.reciprocal(out=inverse[:], in_=norm_of[n][:])
+            q_rows = out_0.rearrange("(p j) m -> p j m", j=TILES)
+            for j in range(TILES):
+                y = y_of[n, j]
+                nc.vector.tensor_scalar_mul(out=y[:], in0=y[:], scalar1=inverse[:, j : j + 1])
+                nc.sync.dma_start(out=q_rows[:, j, :], in_=y[:])
+
+        load("W", W.rearrange("(j p) k -> p j k", p=P))
+        for n in range(LOOKAHEAD - 1):
+            load_batch(n)
+        bias = const.tile([P, D_OUT], BF16, name="bias")
+        nc.scalar.dma_start(out=bias[:], in_=b.partition_broadcast(P))
+        identity = const.tile([P, P], F32, name="identity")
+        make_identity(nc, identity[:])
+        one = const.tile([P, 1], F32, name="one")
+        nc.vector.memset(one[:], 1.0)
+        nc.scalar.sqrt(out=one[:], in_=one[:])
+        membership = const.tile([P, GROUP_SEGMENTS], F32, name="membership")
+        nc.vector.tensor_reduce(
+            out=membership[:],
+            in_=identity[:].rearrange("p (c i) -> p c i", i=SEGMENT_PARTITIONS),
+            axis=mybir.AxisListType.X,
+            op=ADD,
+        )
+        nc.vector.tensor_scalar_mul(out=membership[:], in0=membership[:], scalar1=1.0 / TOKENS)
+
+        transpose("W")
+        regroup("W")
+        new_codes("W", const)
+        for h in range(BANKS):
+            quantise("W", h)
+
+        def in_range(n, end):
+            return 0 <= n < end
+
+        for t in range(-1, batches + SUM_LAG):
+            ahead, behind, summed, stored = t + 1, t - 1, t - SUM_LAG, t - SUM_LAG - 1
+            if in_range(t + LOOKAHEAD, batches):
+                load_batch(t + LOOKAHEAD)
+            if in_range(stored, feature_batches) and stored % BLOCK_BATCHES == BLOCK_BATCHES - 1:
+                store_block(stored // BLOCK_BATCHES)
+            if in_range(ahead, batches):
+                transpose(ahead)
+                regroup(ahead)
+                new_codes(ahead, codes_pool)
+            for pair in range(BATCH_SLICES):
+                for j in range(pair * BANK_TILES, (pair + 1) * BANK_TILES):
+                    if in_range(t, batches):
+                        multiply(t, j)
+                    if j < BANKS and in_range(ahead, batches):
+                        quantise(ahead, j)
+                    if j == 0 and in_range(behind, batches):
+                        norms(behind)
+                    if j == 1 and in_range(behind, feature_batches):
+                        token_weights(behind)
+                    if j == 1 and behind == aspect_batch:
+                        store_q(behind)
+                    if j >= KEPT and in_range(behind, feature_batches):
+                        fold(behind, j - KEPT)
+                if in_range(summed, feature_batches):
+                    group, part = divmod(summed, GROUP_BATCHES)
+                    reduce_tokens(group, part * BATCH_SLICES + pair)
+            if in_range(summed, feature_batches) and summed % BLOCK_BATCHES == BLOCK_BATCHES - 1:
+                collect_block(summed // BLOCK_BATCHES)

@@ -33,8 +33,8 @@ BATCH_SLICES = OUT_SLICES // GROUP_BATCHES
 WORDS = D_IN // 2
 BANK_TILES = 2
 BANKS = TILES // BANK_TILES
-LOOKAHEAD = 4
-SUM_LAG = 3
+ROW_BUFFERS = 4
+SUM_LAG = 4
 TINY = 1e-24
 
 FLOPS = 2 * (512 * 32 + 512) * D_IN * D_OUT
@@ -50,7 +50,7 @@ def tile_linearattention_pa_t_kernel(tc, feature, aspect_v, W, b, out_0, out_1):
     with ExitStack() as ctx:
         ctx.enter_context(tc.manual_schedule())
         const = ctx.enter_context(tc.tile_pool(name="const", bufs=1))
-        rows_pool = ctx.enter_context(tc.tile_pool(name="rows", bufs=LOOKAHEAD))
+        rows_pool = ctx.enter_context(tc.tile_pool(name="rows", bufs=ROW_BUFFERS))
         grouped_pool = ctx.enter_context(tc.tile_pool(name="grouped", bufs=2 * BANKS))
         codes_pool = ctx.enter_context(tc.tile_pool(name="codes", bufs=2))
         y_pool = ctx.enter_context(tc.tile_pool(name="y", bufs=(SUM_LAG + GROUP_BATCHES + 1) * TILES))
@@ -218,7 +218,7 @@ def tile_linearattention_pa_t_kernel(tc, feature, aspect_v, W, b, out_0, out_1):
                 nc.sync.dma_start(out=q_rows[:, j, :], in_=y[:])
 
         load("W", W.rearrange("(j p) k -> p j k", p=P))
-        for n in range(LOOKAHEAD - 1):
+        for n in range(ROW_BUFFERS - 1):
             load_batch(n)
         bias = const.tile([P, D_OUT], BF16, name="bias")
         nc.scalar.dma_start(out=bias[:], in_=b.partition_broadcast(P))
@@ -245,32 +245,35 @@ def tile_linearattention_pa_t_kernel(tc, feature, aspect_v, W, b, out_0, out_1):
         def in_range(n, end):
             return 0 <= n < end
 
-        for t in range(-1, batches + SUM_LAG):
-            ahead, behind, summed, stored = t + 1, t - 1, t - SUM_LAG, t - SUM_LAG - 1
-            if in_range(t + LOOKAHEAD, batches):
-                load_batch(t + LOOKAHEAD)
+        for t in range(-2, batches + SUM_LAG):
+            summed, stored = t - SUM_LAG, t - SUM_LAG - 1
+            if in_range(t + ROW_BUFFERS + 1, batches):
+                load_batch(t + ROW_BUFFERS + 1)
             if in_range(stored, feature_batches) and stored % BLOCK_BATCHES == BLOCK_BATCHES - 1:
                 store_block(stored // BLOCK_BATCHES)
-            if in_range(ahead, batches):
-                transpose(ahead)
-                regroup(ahead)
-                new_codes(ahead, codes_pool)
-            for pair in range(BATCH_SLICES):
-                for j in range(pair * BANK_TILES, (pair + 1) * BANK_TILES):
-                    if in_range(t, batches):
-                        multiply(t, j)
-                    if j < BANKS and in_range(ahead, batches):
-                        quantise(ahead, j)
-                    if j == 0 and in_range(behind, batches):
-                        norms(behind)
-                    if j == 1 and in_range(behind, feature_batches):
-                        token_weights(behind)
-                    if j == 1 and behind == aspect_batch:
-                        store_q(behind)
-                    if j >= KEPT and in_range(behind, feature_batches):
-                        fold(behind, j - KEPT)
+            if in_range(t + 2, batches):
+                transpose(t + 2)
+                regroup(t + 2)
+            if in_range(t + 1, batches):
+                new_codes(t + 1, codes_pool)
+            for half in range(BANKS):
+                first, second = half * BANK_TILES, half * BANK_TILES + 1
+                if in_range(t, batches):
+                    multiply(t, first)
+                if half < FOLDED and in_range(t - 2, feature_batches):
+                    fold(t - 2, half)
+                if in_range(t, batches):
+                    multiply(t, second)
+                if in_range(t + 1, batches):
+                    quantise(t + 1, half)
+                if half == 0 and in_range(t - 1, batches):
+                    norms(t - 1)
+                if half == 1 and in_range(t - 1, feature_batches):
+                    token_weights(t - 1)
+                if half == 1 and t - 1 == aspect_batch:
+                    store_q(t - 1)
                 if in_range(summed, feature_batches):
                     group, part = divmod(summed, GROUP_BATCHES)
-                    reduce_tokens(group, part * BATCH_SLICES + pair)
+                    reduce_tokens(group, part * BATCH_SLICES + half)
             if in_range(summed, feature_batches) and summed % BLOCK_BATCHES == BLOCK_BATCHES - 1:
                 collect_block(summed // BLOCK_BATCHES)

@@ -17,9 +17,6 @@ D_IN = 512
 D_OUT = 512
 TOKENS = 32
 TILES = 4
-FOLDED = 2
-KEPT = TILES - FOLDED
-assert FOLDED <= KEPT
 BATCH_ROWS = TILES * P
 GROUP_BATCHES = 2
 GROUP_TILES = GROUP_BATCHES * TILES
@@ -72,7 +69,6 @@ def tile_linearattention_pa_t_kernel(tc, feature, aspect_v, W, b, out_0, out_1):
         sumsq_of = {}
         norm_of = {}
         weights_of = {}
-        ratio_of = {}
         fm_t_of = {}
         fm_t_sbuf_of = {}
 
@@ -158,24 +154,15 @@ def tile_linearattention_pa_t_kernel(tc, feature, aspect_v, W, b, out_0, out_1):
 
         def token_weights(n):
             inverse = norm_pool.tile([P, TILES], F32, name="inverse")
-            ratio = norm_pool.tile([P, FOLDED], F32, name="ratio")
-            weights = weights_pool.tile([P, KEPT, GROUP_SEGMENTS], F32, name="weights")
+            weights = weights_pool.tile([P, TILES, GROUP_SEGMENTS], F32, name="weights")
             nc.vector.reciprocal(out=inverse[:], in_=norm_of[n][:])
-            nc.vector.tensor_tensor(out=ratio[:], in0=inverse[:, KEPT:], in1=norm_of[n][:, :FOLDED], op=MULT)
             nc.vector.tensor_tensor(
                 out=weights[:],
-                in0=membership[:].unsqueeze(1).to_broadcast([P, KEPT, GROUP_SEGMENTS]),
-                in1=inverse[:, :KEPT].unsqueeze(2).to_broadcast([P, KEPT, GROUP_SEGMENTS]),
+                in0=membership[:].unsqueeze(1).to_broadcast([P, TILES, GROUP_SEGMENTS]),
+                in1=inverse[:].unsqueeze(2).to_broadcast([P, TILES, GROUP_SEGMENTS]),
                 op=MULT,
             )
             weights_of[n] = weights
-            ratio_of[n] = ratio
-
-        def fold(n, i):
-            kept = y_of[n, i]
-            nc.vector.scalar_tensor_tensor(
-                out=kept[:], in0=y_of[n, KEPT + i][:], scalar=ratio_of[n][:, i : i + 1], in1=kept[:], op0=MULT, op1=ADD
-            )
 
         def reduce_tokens(group, s):
             block, place = divmod(group, BLOCK_GROUPS)
@@ -183,15 +170,15 @@ def tile_linearattention_pa_t_kernel(tc, feature, aspect_v, W, b, out_0, out_1):
                 fm_t = fm_t_psum.tile([P, OUT_SLICES * P], F32, name="fm_t")
                 fm_t_of[block] = fm_t
             first = s * P + place * GROUP_SEGMENTS
-            for tile in range(GROUP_BATCHES * KEPT):
-                part, j = divmod(tile, KEPT)
+            for tile in range(GROUP_TILES):
+                part, j = divmod(tile, TILES)
                 n = group * GROUP_BATCHES + part
                 nc.tensor.matmul(
                     out=fm_t_of[block][:, first : first + GROUP_SEGMENTS],
                     lhsT=y_of[n, j][:, s * P : (s + 1) * P],
                     rhs=weights_of[n][:, j, :],
                     start=(tile == 0),
-                    stop=(tile == GROUP_BATCHES * KEPT - 1),
+                    stop=(tile == GROUP_TILES - 1),
                 )
 
         def collect_block(block):
@@ -260,8 +247,6 @@ def tile_linearattention_pa_t_kernel(tc, feature, aspect_v, W, b, out_0, out_1):
                 first, second = half * BANK_TILES, half * BANK_TILES + 1
                 if in_range(t, batches):
                     multiply(t, first)
-                if half < FOLDED and in_range(t - 2, feature_batches):
-                    fold(t - 2, half)
                 if in_range(t, batches):
                     multiply(t, second)
                 if in_range(t + 1, batches):

@@ -10,6 +10,7 @@ U8 = mybir.dt.uint8
 FP8X4 = mybir.dt.float8_e4m3fn_x4
 ADD = mybir.AluOpType.add
 MULT = mybir.AluOpType.mult
+POW = mybir.AluOpType.pow
 SQUARE = mybir.ActivationFunctionType.Square
 
 P = 128
@@ -17,6 +18,9 @@ D_IN = 512
 D_OUT = 512
 TOKENS = 32
 TILES = 4
+FOLDED = 2
+KEPT = TILES - FOLDED
+assert FOLDED <= KEPT
 BATCH_ROWS = TILES * P
 GROUP_BATCHES = 2
 GROUP_TILES = GROUP_BATCHES * TILES
@@ -48,7 +52,7 @@ def tile_linearattention_pa_t_kernel(tc, feature, aspect_v, W, b, out_0, out_1):
         ctx.enter_context(tc.manual_schedule())
         const = ctx.enter_context(tc.tile_pool(name="const", bufs=1))
         rows_pool = ctx.enter_context(tc.tile_pool(name="rows", bufs=ROW_BUFFERS))
-        grouped_pool = ctx.enter_context(tc.tile_pool(name="grouped", bufs=2 * BANKS))
+        grouped_pool = ctx.enter_context(tc.tile_pool(name="grouped", bufs=2))
         codes_pool = ctx.enter_context(tc.tile_pool(name="codes", bufs=2))
         y_pool = ctx.enter_context(tc.tile_pool(name="y", bufs=(SUM_LAG + GROUP_BATCHES + 1) * TILES))
         weights_pool = ctx.enter_context(tc.tile_pool(name="weights", bufs=SUM_LAG + GROUP_BATCHES + 1))
@@ -67,8 +71,10 @@ def tile_linearattention_pa_t_kernel(tc, feature, aspect_v, W, b, out_0, out_1):
         scales_of = {}
         y_of = {}
         sumsq_of = {}
-        norm_of = {}
+        floored_of = {}
+        inverse_of = {}
         weights_of = {}
+        ratio_of = {}
         fm_t_of = {}
         fm_t_sbuf_of = {}
 
@@ -101,28 +107,21 @@ def tile_linearattention_pa_t_kernel(tc, feature, aspect_v, W, b, out_0, out_1):
                 banks_of[n].append(bank)
 
         def regroup(n):
-            grouped_of[n] = []
-            for bank in banks_of[n]:
-                grouped = grouped_pool.tile([P, BANK_TILES * P * 4], BF16, name="grouped", align_bytes=64)
+            grouped = grouped_pool.tile([P, TILES * P * 4], BF16, name="grouped", align_bytes=64)
+            pairs = grouped[:].bitcast(F32).rearrange("p (h j r u) -> p h j r u", h=BANKS, j=BANK_TILES, u=2)
+            for h in range(BANKS):
                 nc.scalar.copy(
-                    out=grouped[:].bitcast(F32).rearrange("p (j r u) -> p j r u", j=BANK_TILES, u=2),
-                    in_=bank[:].rearrange("p (j u r) -> p j r u", j=BANK_TILES, u=2),
+                    out=pairs[:, h],
+                    in_=banks_of[n][h][:].rearrange("p (j u r) -> p j r u", j=BANK_TILES, u=2),
                 )
-                grouped_of[n].append(grouped)
+            grouped_of[n] = grouped
 
-        def new_codes(n, pool):
+        def quantise(n, pool):
             codes = pool.tile([P, TILES * P], U32, name="codes", align_bytes=64)
             scales = pool.tile([P, TILES * P], U8, name="scales", align_bytes=64)
+            nc.vector.quantize_mx(out=codes[:].bitcast(FP8X4), scales=scales[:], in_=grouped_of[n][:])
             codes_of[n] = codes
             scales_of[n] = scales
-
-        def quantise(n, h):
-            cols = slice(h * BANK_TILES * P, (h + 1) * BANK_TILES * P)
-            nc.vector.quantize_mx(
-                out=codes_of[n][:, cols].bitcast(FP8X4),
-                scales=scales_of[n][:, cols],
-                in_=grouped_of[n][h][:],
-            )
 
         def multiply(n, j):
             if j == 0:
@@ -147,22 +146,33 @@ def tile_linearattention_pa_t_kernel(tc, feature, aspect_v, W, b, out_0, out_1):
 
         def norms(n):
             floored = norm_pool.tile([P, TILES], F32, name="floored")
-            norm = norm_pool.tile([P, TILES], F32, name="norm")
-            nc.vector.tensor_scalar_max(out=floored[:], in0=sumsq_of[n][:], scalar1=TINY)
-            nc.scalar.sqrt(out=norm[:], in_=floored[:])
-            norm_of[n] = norm
+            inverse = norm_pool.tile([P, TILES], F32, name="inverse")
+            nc.gpsimd.tensor_scalar_max(out=floored[:], in0=sumsq_of[n][:], scalar1=TINY)
+            nc.gpsimd.tensor_tensor(out=inverse[:], in0=floored[:], in1=minus_half[:], op=POW)
+            floored_of[n] = floored
+            inverse_of[n] = inverse
 
         def token_weights(n):
-            inverse = norm_pool.tile([P, TILES], F32, name="inverse")
-            weights = weights_pool.tile([P, TILES, GROUP_SEGMENTS], F32, name="weights")
-            nc.vector.reciprocal(out=inverse[:], in_=norm_of[n][:])
-            nc.vector.tensor_tensor(
+            inverse = inverse_of[n]
+            norm = norm_pool.tile([P, FOLDED], F32, name="norm")
+            ratio = norm_pool.tile([P, FOLDED], F32, name="ratio")
+            weights = weights_pool.tile([P, KEPT, GROUP_SEGMENTS], F32, name="weights")
+            nc.gpsimd.tensor_tensor(out=norm[:], in0=floored_of[n][:, :FOLDED], in1=inverse[:, :FOLDED], op=MULT)
+            nc.gpsimd.tensor_tensor(out=ratio[:], in0=norm[:], in1=inverse[:, KEPT:], op=MULT)
+            nc.gpsimd.tensor_tensor(
                 out=weights[:],
-                in0=membership[:].unsqueeze(1).to_broadcast([P, TILES, GROUP_SEGMENTS]),
-                in1=inverse[:].unsqueeze(2).to_broadcast([P, TILES, GROUP_SEGMENTS]),
+                in0=membership[:].unsqueeze(1).to_broadcast([P, KEPT, GROUP_SEGMENTS]),
+                in1=inverse[:, :KEPT].unsqueeze(2).to_broadcast([P, KEPT, GROUP_SEGMENTS]),
                 op=MULT,
             )
             weights_of[n] = weights
+            ratio_of[n] = ratio
+
+        def fold(n, i):
+            kept = y_of[n, i]
+            nc.vector.scalar_tensor_tensor(
+                out=kept[:], in0=y_of[n, KEPT + i][:], scalar=ratio_of[n][:, i : i + 1], in1=kept[:], op0=MULT, op1=ADD
+            )
 
         def reduce_tokens(group, s):
             block, place = divmod(group, BLOCK_GROUPS)
@@ -170,15 +180,15 @@ def tile_linearattention_pa_t_kernel(tc, feature, aspect_v, W, b, out_0, out_1):
                 fm_t = fm_t_psum.tile([P, OUT_SLICES * P], F32, name="fm_t")
                 fm_t_of[block] = fm_t
             first = s * P + place * GROUP_SEGMENTS
-            for tile in range(GROUP_TILES):
-                part, j = divmod(tile, TILES)
+            for tile in range(GROUP_BATCHES * KEPT):
+                part, j = divmod(tile, KEPT)
                 n = group * GROUP_BATCHES + part
                 nc.tensor.matmul(
                     out=fm_t_of[block][:, first : first + GROUP_SEGMENTS],
                     lhsT=y_of[n, j][:, s * P : (s + 1) * P],
                     rhs=weights_of[n][:, j, :],
                     start=(tile == 0),
-                    stop=(tile == GROUP_TILES - 1),
+                    stop=(tile == GROUP_BATCHES * KEPT - 1),
                 )
 
         def collect_block(block):
@@ -196,8 +206,7 @@ def tile_linearattention_pa_t_kernel(tc, feature, aspect_v, W, b, out_0, out_1):
             nc.sync.dma_start(out=out_1[block * P : (block + 1) * P, :], in_=fm[:])
 
         def store_q(n):
-            inverse = norm_pool.tile([P, TILES], F32, name="inverse")
-            nc.vector.reciprocal(out=inverse[:], in_=norm_of[n][:])
+            inverse = inverse_of[n]
             q_rows = out_0.rearrange("(p j) m -> p j m", j=TILES)
             for j in range(TILES):
                 y = y_of[n, j]
@@ -211,9 +220,8 @@ def tile_linearattention_pa_t_kernel(tc, feature, aspect_v, W, b, out_0, out_1):
         nc.scalar.dma_start(out=bias[:], in_=b.partition_broadcast(P))
         identity = const.tile([P, P], F32, name="identity")
         make_identity(nc, identity[:])
-        one = const.tile([P, 1], F32, name="one")
-        nc.vector.memset(one[:], 1.0)
-        nc.scalar.sqrt(out=one[:], in_=one[:])
+        minus_half = const.tile([P, TILES], F32, name="minus_half")
+        nc.vector.memset(minus_half[:], -0.5)
         membership = const.tile([P, GROUP_SEGMENTS], F32, name="membership")
         nc.vector.tensor_reduce(
             out=membership[:],
@@ -225,9 +233,7 @@ def tile_linearattention_pa_t_kernel(tc, feature, aspect_v, W, b, out_0, out_1):
 
         transpose("W")
         regroup("W")
-        new_codes("W", const)
-        for h in range(BANKS):
-            quantise("W", h)
+        quantise("W", const)
 
         def in_range(n, end):
             return 0 <= n < end
@@ -241,20 +247,20 @@ def tile_linearattention_pa_t_kernel(tc, feature, aspect_v, W, b, out_0, out_1):
             if in_range(t + 2, batches):
                 transpose(t + 2)
                 regroup(t + 2)
-            if in_range(t + 1, batches):
-                new_codes(t + 1, codes_pool)
+            if in_range(t - 1, batches):
+                norms(t - 1)
+            if in_range(t - 1, feature_batches):
+                token_weights(t - 1)
             for half in range(BANKS):
                 first, second = half * BANK_TILES, half * BANK_TILES + 1
                 if in_range(t, batches):
                     multiply(t, first)
+                if half < FOLDED and in_range(t - 2, feature_batches):
+                    fold(t - 2, half)
                 if in_range(t, batches):
                     multiply(t, second)
-                if in_range(t + 1, batches):
-                    quantise(t + 1, half)
-                if half == 0 and in_range(t - 1, batches):
-                    norms(t - 1)
-                if half == 1 and in_range(t - 1, feature_batches):
-                    token_weights(t - 1)
+                if half == 0 and in_range(t + 1, batches):
+                    quantise(t + 1, codes_pool)
                 if half == 1 and t - 1 == aspect_batch:
                     store_q(t - 1)
                 if in_range(summed, feature_batches):

from contextlib import ExitStack

import concourse.mybir as mybir
from concourse.masks import make_identity

F32 = mybir.dt.float32
BF16 = mybir.dt.bfloat16
U32 = mybir.dt.uint32
U8 = mybir.dt.uint8
FP8X4 = mybir.dt.float8_e4m3fn_x4
ADD = mybir.AluOpType.add
MULT = mybir.AluOpType.mult
POW = mybir.AluOpType.pow
SQUARE = mybir.ActivationFunctionType.Square

P = 128
D_IN = 512
D_OUT = 512
TOKENS = 32
TILES = 4
FOLDED = 2
KEPT = TILES - FOLDED
assert FOLDED <= KEPT
BATCH_ROWS = TILES * P
GROUP_BATCHES = 2
GROUP_TILES = GROUP_BATCHES * TILES
GROUP_ROWS = GROUP_TILES * P
GROUP_SEGMENTS = GROUP_ROWS // TOKENS
SEGMENT_PARTITIONS = TOKENS // GROUP_TILES
BLOCK_GROUPS = P // GROUP_SEGMENTS
BLOCK_BATCHES = BLOCK_GROUPS * GROUP_BATCHES
OUT_SLICES = D_OUT // P
BATCH_SLICES = OUT_SLICES // GROUP_BATCHES
WORDS = D_IN // 2
BANK_TILES = 2
BANKS = TILES // BANK_TILES
ROW_BUFFERS = 4
SUM_LAG = 4
TINY = 1e-24

FLOPS = 2 * (512 * 32 + 512) * D_IN * D_OUT


def tile_linearattention_pa_t_kernel(tc, feature, aspect_v, W, b, out_0, out_1):
    nc = tc.nc
    tokens = feature.flatten_outer_dims()
    feature_batches = tokens.shape[0] // BATCH_ROWS
    aspect_batch = feature_batches
    batches = feature_batches + 1

    with ExitStack() as ctx:
        ctx.enter_context(tc.manual_schedule())
        const = ctx.enter_context(tc.tile_pool(name="const", bufs=1))
        rows_pool = ctx.enter_context(tc.tile_pool(name="rows", bufs=ROW_BUFFERS))
        grouped_pool = ctx.enter_context(tc.tile_pool(name="grouped", bufs=2))
        codes_pool = ctx.enter_context(tc.tile_pool(name="codes", bufs=2))
        y_pool = ctx.enter_context(tc.tile_pool(name="y", bufs=(SUM_LAG + GROUP_BATCHES + 1) * TILES))
        weights_pool = ctx.enter_context(tc.tile_pool(name="weights", bufs=SUM_LAG + GROUP_BATCHES + 1))
        squares_pool = ctx.enter_context(tc.tile_pool(name="squares", bufs=TILES))
        norm_pool = ctx.enter_context(tc.tile_pool(name="norm", bufs=3))
        fm_pool = ctx.enter_context(tc.tile_pool(name="fm", bufs=2))
        words_psum = ctx.enter_context(tc.psum_pool(name="words_psum", bufs=BANKS))
        product_psum = ctx.enter_context(tc.psum_pool(name="product_psum", bufs=TILES))
        fm_t_psum = ctx.enter_context(tc.psum_pool(name="fm_t_psum", bufs=1))
        fm_psum = ctx.enter_context(tc.psum_pool(name="fm_psum", bufs=1))

        rows_of = {}
        banks_of = {}
        grouped_of = {}
        codes_of = {}
        scales_of = {}
        y_of = {}
        sumsq_of = {}
        floored_of = {}
        inverse_of = {}
        weights_of = {}
        ratio_of = {}
        fm_t_of = {}
        fm_t_sbuf_of = {}

        def load(n, dram_view):
            rows = rows_pool.tile([P, TILES * D_IN], BF16, name="rows")
            nc.sync.dma_start(out=rows[:].rearrange("p (j k) -> p j k", j=TILES), in_=dram_view)
            rows_of[n] = rows

        def load_batch(n):
            if n == aspect_batch:
                load(n, aspect_v.rearrange("(p j) k -> p j k", j=TILES))
            else:
                group, part = divmod(n, GROUP_BATCHES)
                group_rows = tokens[group * GROUP_ROWS : (group + 1) * GROUP_ROWS, :]
                by_partition = group_rows.rearrange("(p j) k -> p j k", j=GROUP_TILES)
                load(n, by_partition[:, part * TILES : (part + 1) * TILES, :])

        def transpose(n):
            words = rows_of[n][:].bitcast(F32)
            blocks = BANK_TILES * WORDS // P
            banks_of[n] = []
            for h in range(BANKS):
                bank = words_psum.tile([P, BANK_TILES * WORDS], F32, name="bank")
                for block in range(blocks):
                    nc.tensor.transpose(
                        out=bank[:, block * P : (block + 1) * P],
                        in_=words[:, (h * blocks + block) * P : (h * blocks + block + 1) * P],
                        identity=identity[:],
                    )
                banks_of[n].append(bank)

        def regroup(n):
            grouped = grouped_pool.tile([P, TILES * P * 4], BF16, name="grouped", align_bytes=64)
            pairs = grouped[:].bitcast(F32).rearrange("p (h j r u) -> p h j r u", h=BANKS, j=BANK_TILES, u=2)
            for h in range(BANKS):
                nc.scalar.copy(
                    out=pairs[:, h],
                    in_=banks_of[n][h][:].rearrange("p (j u r) -> p j r u", j=BANK_TILES, u=2),
                )
            grouped_of[n] = grouped

        def quantise(n, pool):
            codes = pool.tile([P, TILES * P], U32, name="codes", align_bytes=64)
            scales = pool.tile([P, TILES * P], U8, name="scales", align_bytes=64)
            nc.vector.quantize_mx(out=codes[:].bitcast(FP8X4), scales=scales[:], in_=grouped_of[n][:])
            codes_of[n] = codes
            scales_of[n] = scales

        def multiply(n, j):
            if j == 0:
                sumsq = norm_pool.tile([P, TILES], F32, name="sumsq")
                sumsq_of[n] = sumsq
            cols = slice(j * P, (j + 1) * P)
            product = product_psum.tile([P, D_OUT], F32, name="product")
            nc.tensor.matmul_mx(
                out=product[:],
                lhsT=codes_of[n][:, cols].bitcast(FP8X4),
                lhsT_scale=scales_of[n][:, cols],
                rhs=codes_of["W"][:].bitcast(FP8X4),
                rhs_scale=scales_of["W"][:],
                start=True,
                stop=True,
            )
            y = y_pool.tile([P, D_OUT], F32, name="y")
            y_of[n, j] = y
            nc.vector.tensor_tensor(out=y[:], in0=product[:], in1=bias[:], op=ADD)
            squares = squares_pool.tile([P, D_OUT], BF16, name="squares")
            nc.scalar.activation(out=squares[:], in_=y[:], func=SQUARE, accum_out=sumsq_of[n][:, j : j + 1])

        def norms(n):
            floored = norm_pool.tile([P, TILES], F32, name="floored")
            inverse = norm_pool.tile([P, TILES], F32, name="inverse")
            nc.gpsimd.tensor_scalar_max(out=floored[:], in0=sumsq_of[n][:], scalar1=TINY)
            nc.gpsimd.tensor_tensor(out=inverse[:], in0=floored[:], in1=minus_half[:], op=POW)
            floored_of[n] = floored
            inverse_of[n] = inverse

        def token_weights(n):
            inverse = inverse_of[n]
            norm = norm_pool.tile([P, FOLDED], F32, name="norm")
            ratio = norm_pool.tile([P, FOLDED], F32, name="ratio")
            weights = weights_pool.tile([P, KEPT, GROUP_SEGMENTS], F32, name="weights")
            nc.gpsimd.tensor_tensor(out=norm[:], in0=floored_of[n][:, :FOLDED], in1=inverse[:, :FOLDED], op=MULT)
            nc.gpsimd.tensor_tensor(out=ratio[:], in0=norm[:], in1=inverse[:, KEPT:], op=MULT)
            nc.gpsimd.tensor_tensor(
                out=weights[:],
                in0=membership[:].unsqueeze(1).to_broadcast([P, KEPT, GROUP_SEGMENTS]),
                in1=inverse[:, :KEPT].unsqueeze(2).to_broadcast([P, KEPT, GROUP_SEGMENTS]),
                op=MULT,
            )
            weights_of[n] = weights
            ratio_of[n] = ratio

        def fold(n, i):
            kept = y_of[n, i]
            nc.vector.scalar_tensor_tensor(
                out=kept[:], in0=y_of[n, KEPT + i][:], scalar=ratio_of[n][:, i : i + 1], in1=kept[:], op0=MULT, op1=ADD
            )

        def reduce_tokens(group, s):
            block, place = divmod(group, BLOCK_GROUPS)
            if place == 0 and s == 0:
                fm_t = fm_t_psum.tile([P, OUT_SLICES * P], F32, name="fm_t")
                fm_t_of[block] = fm_t
            first = s * P + place * GROUP_SEGMENTS
            for tile in range(GROUP_BATCHES * KEPT):
                part, j = divmod(tile, KEPT)
                n = group * GROUP_BATCHES + part
                nc.tensor.matmul(
                    out=fm_t_of[block][:, first : first + GROUP_SEGMENTS],
                    lhsT=y_of[n, j][:, s * P : (s + 1) * P],
                    rhs=weights_of[n][:, j, :],
                    start=(tile == 0),
                    stop=(tile == GROUP_BATCHES * KEPT - 1),
                )

        def collect_block(block):
            fm_t_sbuf = fm_pool.tile([P, OUT_SLICES * P], F32, name="fm_t_sbuf")
            nc.vector.tensor_copy(out=fm_t_sbuf[:], in_=fm_t_of[block][:])
            fm_t_sbuf_of[block] = fm_t_sbuf

        def store_block(block):
            fm_bank = fm_psum.tile([P, D_OUT], F32, name="fm_bank")
            for s in range(OUT_SLICES):
                cols = slice(s * P, (s + 1) * P)
                nc.tensor.transpose(out=fm_bank[:, cols], in_=fm_t_sbuf_of[block][:, cols], identity=identity[:])
            fm = fm_pool.tile([P, D_OUT], F32, name="fm")
            nc.scalar.copy(out=fm[:], in_=fm_bank[:])
            nc.sync.dma_start(out=out_1[block * P : (block + 1) * P, :], in_=fm[:])

        def store_q(n):
            inverse = inverse_of[n]
            q_rows = out_0.rearrange("(p j) m -> p j m", j=TILES)
            for j in range(TILES):
                y = y_of[n, j]
                nc.vector.tensor_scalar_mul(out=y[:], in0=y[:], scalar1=inverse[:, j : j + 1])
                nc.sync.dma_start(out=q_rows[:, j, :], in_=y[:])

        load("W", W.rearrange("(j p) k -> p j k", p=P))
        for n in range(ROW_BUFFERS - 1):
            load_batch(n)
        bias = const.tile([P, D_OUT], BF16, name="bias")
        nc.scalar.dma_start(out=bias[:], in_=b.partition_broadcast(P))
        identity = const.tile([P, P], F32, name="identity")
        make_identity(nc, identity[:])
        minus_half = const.tile([P, TILES], F32, name="minus_half")
        nc.vector.memset(minus_half[:], -0.5)
        membership = const.tile([P, GROUP_SEGMENTS], F32, name="membership")
        nc.vector.tensor_reduce(
            out=membership[:],
            in_=identity[:].rearrange("p (c i) -> p c i", i=SEGMENT_PARTITIONS),
            axis=mybir.AxisListType.X,
            op=ADD,
        )
        nc.vector.tensor_scalar_mul(out=membership[:], in0=membership[:], scalar1=1.0 / TOKENS)

        transpose("W")
        regroup("W")
        quantise("W", const)

        def in_range(n, end):
            return 0 <= n < end

        for t in range(-2, batches + SUM_LAG):
            summed, stored = t - SUM_LAG, t - SUM_LAG - 1
            if in_range(t + ROW_BUFFERS + 1, batches):
                load_batch(t + ROW_BUFFERS + 1)
            if in_range(stored, feature_batches) and stored % BLOCK_BATCHES == BLOCK_BATCHES - 1:
                store_block(stored // BLOCK_BATCHES)
            if in_range(t + 2, batches):
                transpose(t + 2)
                regroup(t + 2)
            if in_range(t - 1, batches):
                norms(t - 1)
            if in_range(t - 1, feature_batches):
                token_weights(t - 1)
            for half in range(BANKS):
                first, second = half * BANK_TILES, half * BANK_TILES + 1
                if in_range(t, batches):
                    multiply(t, first)
                if half < FOLDED and in_range(t - 2, feature_batches):
                    fold(t - 2, half)
                if in_range(t, batches):
                    multiply(t, second)
                if half == 0 and in_range(t + 1, batches):
                    quantise(t + 1, codes_pool)
                if half == 1 and t - 1 == aspect_batch:
                    store_q(t - 1)
                if in_range(summed, feature_batches):
                    group, part = divmod(summed, GROUP_BATCHES)
                    reduce_tokens(group, part * BATCH_SLICES + half)
            if in_range(summed, feature_batches) and summed % BLOCK_BATCHES == BLOCK_BATCHES - 1:
                collect_block(summed // BLOCK_BATCHES)
